import numpy as np
import ml_dtypes


def mxq(x, axis, fmt="e4m3"):
    dtype, down = {"e4m3": (ml_dtypes.float8_e4m3fn, 7), "e5m2": (ml_dtypes.float8_e5m2, 14)}[fmt]
    v = np.moveaxis(np.asarray(x, np.float32).astype(ml_dtypes.bfloat16).astype(np.float64), axis, -1)
    blocks = v.reshape(v.shape[:-1] + (-1, 32))
    amax = np.abs(blocks).max(-1, keepdims=True)
    byte = np.maximum(np.where(amax > 0, np.frexp(amax)[1] - 1 + 127, 0) - down, 1)
    scale = np.exp2(byte - 127.0)
    codes = (blocks / scale).astype(np.float32).astype(dtype).astype(np.float64)
    return np.moveaxis((codes * scale).reshape(v.shape), -1, axis)


WIDE = False


def mx_kscale(k):
    if not WIDE:
        return np.ones(k)
    levels = np.array([10, -10, 5, -5, 0])
    a = np.random.permutation(np.resize(levels, k // 512 * 4)).reshape(k // 512, 4)
    idx = np.arange(k)
    return np.exp2(a[idx // 512, idx % 128 // 32])


BF16 = ml_dtypes.bfloat16


def bf(x):
    return np.asarray(x, np.float32).astype(BF16)


def f64(x):
    return np.asarray(x).astype(np.float64)


B, L, E, H, DH, RK, RD, MAXLEN = 4, 128, 2048, 16, 128, 512, 128, 4096


def apply_rope(x, cos, sin):
    cos = cos[None, :, None, :]
    sin = sin[None, :, None, :]
    x1, x2 = x[..., 0::2], x[..., 1::2]
    out_real = x1 * cos - x2 * sin
    out_imag = x1 * sin + x2 * cos
    return np.stack([out_real, out_imag], axis=-1).reshape(x.shape)


def setup_inputs():
    s = mx_kscale(E)
    return {"x": bf(np.random.standard_normal((B, L, E)) * s),
            "cos": bf(np.random.uniform(size=(L, RD // 2))),
            "sin": bf(np.random.uniform(size=(L, RD // 2))),
            "wq": bf(np.random.standard_normal((E, H * (DH + RD))) / np.sqrt(E) / s[:, None])}


def reference(x, cos, sin, wq):
    q_all = (mxq(f64(x), 2, "e4m3") @ mxq(f64(wq), 0, "e4m3")).reshape(B, L, H, DH + RD)
    q_head, q_rope = q_all[..., :DH], q_all[..., DH:]
    q_rope = apply_rope(q_rope, f64(cos), f64(sin))
    return np.concatenate([q_head, q_rope], axis=-1)

@@ -1,0 +1,197 @@
+from contextlib import ExitStack
+
+import concourse.mybir as mybir
+from concourse.masks import make_identity
+
+F32 = mybir.dt.float32
+BF16 = mybir.dt.bfloat16
+U32 = mybir.dt.uint32
+U8 = mybir.dt.uint8
+FP8X4 = mybir.dt.float8_e4m3fn_x4
+MULT = mybir.AluOpType.mult
+ADD = mybir.AluOpType.add
+
+P = 128
+PACK = 4
+K_PASS = P * PACK
+
+BATCH, SEQ, EMBED = 4, 128, 2048
+HEADS, D_CONTENT, D_ROPE = 16, 128, 128
+D_HEAD = D_CONTENT + D_ROPE
+PAIRS = D_ROPE // 2
+PASSES = EMBED // K_PASS
+
+BLOCK_HEADS = 4
+BLOCK_COLS = BLOCK_HEADS * D_HEAD
+BLOCKS = HEADS // BLOCK_HEADS
+TILE_COLS = BLOCK_HEADS * D_ROPE
+CONTENT, ROPE = 0, 1
+RUN = 4
+
+VECTOR_HEADS = 1
+BLOCKS_AHEAD = 3
+
+FLOPS = 2 * BATCH * SEQ * EMBED * HEADS * D_HEAD
+
+
+def tile_multiheadlatentattention_pb_kernel(tc, x, cos, sin, wq, out):
+    nc = tc.nc
+    wq_rows = wq.rearrange("(c p j) n -> c p j n", p=P, j=PACK)
+
+    with ExitStack() as ctx:
+        const = ctx.enter_context(tc.tile_pool(name="const", bufs=1))
+        x_pool = ctx.enter_context(tc.tile_pool(name="x_pool", bufs=BATCH))
+        w_pool = ctx.enter_context(tc.tile_pool(name="w_pool", bufs=BLOCKS_AHEAD * PASSES))
+        grouped_pool = ctx.enter_context(tc.tile_pool(name="grouped_pool", bufs=4))
+        codes_pool = ctx.enter_context(tc.tile_pool(name="codes_pool", bufs=3))
+        term_pool = ctx.enter_context(tc.tile_pool(name="term_pool", bufs=3))
+        q_pool = ctx.enter_context(tc.tile_pool(name="q_pool", bufs=2 * BATCH))
+        psum = ctx.enter_context(tc.psum_pool(name="psum", bufs=8))
+
+        def load_w_chunk(block, c):
+            w_chunk = w_pool.tile([P, PACK, BLOCK_COLS], BF16)
+            cols = slice(block * BLOCK_COLS, (block + 1) * BLOCK_COLS)
+            nc.sync.dma_start(out=w_chunk[:], in_=wq_rows[c, :, :, cols])
+            return w_chunk
+
+        w_chunks = {}
+        w_chunks[(0, 0)] = load_w_chunk(0, 0)
+        x_tiles = []
+        for b in range(BATCH):
+            x_rows = x_pool.tile([P, EMBED], BF16)
+            nc.sync.dma_start(out=x_rows[:], in_=x[b])
+            x_tiles.append(x_rows)
+        for block in range(BLOCKS_AHEAD):
+            for c in range(PASSES):
+                if (block, c) != (0, 0):
+                    w_chunks[(block, c)] = load_w_chunk(block, c)
+
+        cos_rows = const.tile([P, PAIRS], BF16)
+        nc.scalar.dma_start(out=cos_rows[:], in_=cos)
+        sin_rows = const.tile([P, PAIRS], BF16)
+        nc.scalar.dma_start(out=sin_rows[:], in_=sin)
+
+        cos_pairs = const.tile([P, PAIRS, 2], F32)
+        nc.vector.tensor_copy(
+            out=cos_pairs[:], in_=cos_rows[:].unsqueeze(2).to_broadcast([P, PAIRS, 2])
+        )
+        sin_signed = const.tile([P, 2, PAIRS], F32)
+        nc.vector.tensor_scalar_mul(out=sin_signed[:, 0, :], in0=sin_rows[:], scalar1=-1.0)
+        nc.vector.tensor_copy(out=sin_signed[:, 1, :], in_=sin_rows[:])
+
+        identity = const.tile([P, P], F32)
+        make_identity(nc, identity[:])
+
+        x_codes = const.tile([P, BATCH, PASSES, SEQ], U32, align_bytes=64)
+        x_scales = const.tile([P, BATCH, PASSES, SEQ], U8, align_bytes=64)
+        for b in range(BATCH):
+            x_words = x_tiles[b][:].bitcast(F32).rearrange("r (c q u) -> r c u q", c=PASSES, u=2)
+            x_grouped = x_pool.tile([P, EMBED], BF16, bufs=2, align_bytes=64)
+            grouped_words = x_grouped[:].bitcast(F32).rearrange(
+                "p (c r u) -> p c r u", c=PASSES, u=2
+            )
+            for first in range(0, PASSES, 2):
+                flipped = psum.tile([P, 2, 2, SEQ], F32, tag="bank")
+                for c in range(2):
+                    for u in range(2):
+                        nc.tensor.transpose(
+                            flipped[:, c, u, :], x_words[:, first + c, u, :], identity[:]
+                        )
+                nc.vector.tensor_copy(
+                    out=grouped_words[:, first : first + 2],
+                    in_=flipped[:].rearrange("p c u r -> p c r u"),
+                )
+            nc.vector.quantize_mx(
+                out=x_codes[:, b].rearrange("p c r -> p (c r)").bitcast(FP8X4),
+                scales=x_scales[:, b].rearrange("p c r -> p (c r)"),
+                in_=x_grouped[:],
+            )
+
+        def regroup(copy, w_chunk, kind, w_grouped, heads):
+            source = w_chunk[:].rearrange(
+                "p j (h kind g i) -> p h kind g j i", h=BLOCK_HEADS, kind=2, i=RUN
+            )
+            target = w_grouped[:].rearrange(
+                "p (h g i j) -> p h g j i", h=BLOCK_HEADS, i=RUN, j=PACK
+            )
+            copy(out=target[:, heads], in_=source[:, heads, kind])
+
+        def rotate(bank, q_rows):
+            by_head = bank[:].rearrange("p (h d) -> p h d", h=BLOCK_HEADS)
+            by_pair = bank[:].rearrange("p (h j two) -> p h j two", h=BLOCK_HEADS, two=2)
+            cos_term = term_pool.tile([P, BLOCK_HEADS, PAIRS, 2], F32)
+            nc.vector.tensor_tensor(
+                out=cos_term[:].rearrange("p h j two -> p h (j two)"),
+                in0=by_head,
+                in1=cos_pairs[:]
+                .rearrange("p j two -> p (j two)")
+                .unsqueeze(1)
+                .to_broadcast([P, BLOCK_HEADS, D_ROPE]),
+                op=MULT,
+            )
+            sin_term = term_pool.tile([P, 2, BLOCK_HEADS, PAIRS], F32)
+            for two in range(2):
+                nc.vector.tensor_tensor(
+                    out=sin_term[:, two],
+                    in0=by_pair[:, :, :, 1 - two],
+                    in1=sin_signed[:, two, :].unsqueeze(1).to_broadcast([P, BLOCK_HEADS, PAIRS]),
+                    op=MULT,
+                )
+            nc.vector.tensor_tensor(
+                out=q_rows[:, :, D_CONTENT:].rearrange("p h (j two) -> p h j two", two=2),
+                in0=cos_term[:],
+                in1=sin_term[:].rearrange("p two h j -> p h j two"),
+                op=ADD,
+            )
+
+        for block in range(BLOCKS):
+            q_tiles = []
+            for b in range(BATCH):
+                q_rows = q_pool.tile([P, BLOCK_HEADS, D_HEAD], F32)
+                q_tiles.append(q_rows)
+
+            for kind in (ROPE, CONTENT):
+                w_codes = codes_pool.tile([P, PASSES, TILE_COLS], U32, align_bytes=64)
+                w_scales = codes_pool.tile([P, PASSES, TILE_COLS], U8, align_bytes=64)
+                banks = []
+                for b in range(BATCH):
+                    bank = psum.tile([P, TILE_COLS], F32, tag="bank")
+                    banks.append(bank)
+
+                for c in range(PASSES):
+                    w_grouped = grouped_pool.tile([P, TILE_COLS * PACK], BF16, align_bytes=64)
+                    w_chunk = w_chunks[(block, c)]
+                    regroup(nc.vector.tensor_copy, w_chunk, kind, w_grouped, slice(0, VECTOR_HEADS))
+                    regroup(nc.scalar.copy, w_chunk, kind, w_grouped, slice(VECTOR_HEADS, BLOCK_HEADS))
+                    nc.vector.quantize_mx(
+                        out=w_codes[:, c, :].bitcast(FP8X4),
+                        scales=w_scales[:, c, :],
+                        in_=w_grouped[:],
+                    )
+                    for b in range(BATCH):
+                        nc.tensor.matmul_mx(
+                            out=banks[b][:],
+                            lhsT=x_codes[:, b, c, :].bitcast(FP8X4),
+                            lhsT_scale=x_scales[:, b, c, :],
+                            rhs=w_codes[:, c, :].bitcast(FP8X4),
+                            rhs_scale=w_scales[:, c, :],
+                            start=(c == 0),
+                            stop=(c == PASSES - 1),
+                        )
+
+                for b in range(BATCH):
+                    if kind == ROPE:
+                        rotate(banks[b], q_tiles[b])
+                    else:
+                        nc.scalar.copy(
+                            out=q_tiles[b][:, :, :D_CONTENT],
+                            in_=banks[b][:].rearrange("p (h d) -> p h d", h=BLOCK_HEADS),
+                        )
+
+            heads = slice(block * BLOCK_HEADS, (block + 1) * BLOCK_HEADS)
+            for b in range(BATCH):
+                nc.sync.dma_start(out=out[b, :, heads, :], in_=q_tiles[b][:])
+
+            if block + BLOCKS_AHEAD < BLOCKS:
+                for c in range(PASSES):
+                    w_chunks[(block + BLOCKS_AHEAD, c)] = load_w_chunk(block + BLOCKS_AHEAD, c)

@@ -29,92 +29,88 @@ CONTENT, ROPE = 0, 1
 RUN = 4
 
 VECTOR_HEADS = 1
+REGROUP_AHEAD = 3
 BLOCKS_AHEAD = 3
 
 FLOPS = 2 * BATCH * SEQ * EMBED * HEADS * D_HEAD
+
+assert BATCH == PASSES
 
 
 def tile_multiheadlatentattention_pb_kernel(tc, x, cos, sin, wq, out):
     nc = tc.nc
     wq_rows = wq.rearrange("(c p j) n -> c p j n", p=P, j=PACK)
 
+    units = [
+        (block, kind, c)
+        for block in range(BLOCKS)
+        for kind in (ROPE, CONTENT)
+        for c in range(PASSES)
+    ]
+
     with ExitStack() as ctx:
         const = ctx.enter_context(tc.tile_pool(name="const", bufs=1))
         x_pool = ctx.enter_context(tc.tile_pool(name="x_pool", bufs=BATCH))
         w_pool = ctx.enter_context(tc.tile_pool(name="w_pool", bufs=BLOCKS_AHEAD * PASSES))
-        grouped_pool = ctx.enter_context(tc.tile_pool(name="grouped_pool", bufs=4))
+        grouped_pool = ctx.enter_context(tc.tile_pool(name="grouped_pool", bufs=REGROUP_AHEAD + 2))
         codes_pool = ctx.enter_context(tc.tile_pool(name="codes_pool", bufs=3))
         term_pool = ctx.enter_context(tc.tile_pool(name="term_pool", bufs=3))
         q_pool = ctx.enter_context(tc.tile_pool(name="q_pool", bufs=2 * BATCH))
         psum = ctx.enter_context(tc.psum_pool(name="psum", bufs=8))
+        ctx.enter_context(tc.manual_schedule())
+
+        w_chunks = {}
+        w_grouped = {}
+        w_codes = {}
+        w_scales = {}
+        banks = {}
+        q_tiles = {}
 
         def load_w_chunk(block, c):
             w_chunk = w_pool.tile([P, PACK, BLOCK_COLS], BF16)
             cols = slice(block * BLOCK_COLS, (block + 1) * BLOCK_COLS)
             nc.sync.dma_start(out=w_chunk[:], in_=wq_rows[c, :, :, cols])
-            return w_chunk
+            w_chunks[(block, c)] = w_chunk
 
-        w_chunks = {}
-        w_chunks[(0, 0)] = load_w_chunk(0, 0)
-        x_tiles = []
-        for b in range(BATCH):
-            x_rows = x_pool.tile([P, EMBED], BF16)
-            nc.sync.dma_start(out=x_rows[:], in_=x[b])
-            x_tiles.append(x_rows)
-        for block in range(BLOCKS_AHEAD):
-            for c in range(PASSES):
-                if (block, c) != (0, 0):
-                    w_chunks[(block, c)] = load_w_chunk(block, c)
-
-        cos_rows = const.tile([P, PAIRS], BF16)
-        nc.scalar.dma_start(out=cos_rows[:], in_=cos)
-        sin_rows = const.tile([P, PAIRS], BF16)
-        nc.scalar.dma_start(out=sin_rows[:], in_=sin)
-
-        cos_pairs = const.tile([P, PAIRS, 2], F32)
-        nc.vector.tensor_copy(
-            out=cos_pairs[:], in_=cos_rows[:].unsqueeze(2).to_broadcast([P, PAIRS, 2])
-        )
-        sin_signed = const.tile([P, 2, PAIRS], F32)
-        nc.vector.tensor_scalar_mul(out=sin_signed[:, 0, :], in0=sin_rows[:], scalar1=-1.0)
-        nc.vector.tensor_copy(out=sin_signed[:, 1, :], in_=sin_rows[:])
-
-        identity = const.tile([P, P], F32)
-        make_identity(nc, identity[:])
-
-        x_codes = const.tile([P, BATCH, PASSES, SEQ], U32, align_bytes=64)
-        x_scales = const.tile([P, BATCH, PASSES, SEQ], U8, align_bytes=64)
-        for b in range(BATCH):
-            x_words = x_tiles[b][:].bitcast(F32).rearrange("r (c q u) -> r c u q", c=PASSES, u=2)
-            x_grouped = x_pool.tile([P, EMBED], BF16, bufs=2, align_bytes=64)
-            grouped_words = x_grouped[:].bitcast(F32).rearrange(
-                "p (c r u) -> p c r u", c=PASSES, u=2
-            )
-            for first in range(0, PASSES, 2):
-                flipped = psum.tile([P, 2, 2, SEQ], F32, tag="bank")
-                for c in range(2):
-                    for u in range(2):
-                        nc.tensor.transpose(
-                            flipped[:, c, u, :], x_words[:, first + c, u, :], identity[:]
-                        )
-                nc.vector.tensor_copy(
-                    out=grouped_words[:, first : first + 2],
-                    in_=flipped[:].rearrange("p c u r -> p c r u"),
-                )
-            nc.vector.quantize_mx(
-                out=x_codes[:, b].rearrange("p c r -> p (c r)").bitcast(FP8X4),
-                scales=x_scales[:, b].rearrange("p c r -> p (c r)"),
-                in_=x_grouped[:],
-            )
-
-        def regroup(copy, w_chunk, kind, w_grouped, heads):
-            source = w_chunk[:].rearrange(
+        def regroup(unit):
+            block, kind, c = unit
+            grouped = grouped_pool.tile([P, TILE_COLS * PACK], BF16, align_bytes=64)
+            source = w_chunks[(block, c)][:].rearrange(
                 "p j (h kind g i) -> p h kind g j i", h=BLOCK_HEADS, kind=2, i=RUN
             )
-            target = w_grouped[:].rearrange(
-                "p (h g i j) -> p h g j i", h=BLOCK_HEADS, i=RUN, j=PACK
+            target = grouped[:].rearrange("p (h g i j) -> p h g j i", h=BLOCK_HEADS, i=RUN, j=PACK)
+            nc.vector.tensor_copy(out=target[:, :VECTOR_HEADS], in_=source[:, :VECTOR_HEADS, kind])
+            nc.scalar.copy(out=target[:, VECTOR_HEADS:], in_=source[:, VECTOR_HEADS:, kind])
+            w_grouped[unit] = grouped
+            if kind == CONTENT and block + BLOCKS_AHEAD < BLOCKS:
+                load_w_chunk(block + BLOCKS_AHEAD, c)
+
+        def quantise_and_multiply(unit):
+            block, kind, c = unit
+            if c == 0:
+                codes = codes_pool.tile([P, PASSES, TILE_COLS], U32, align_bytes=64)
+                scales = codes_pool.tile([P, PASSES, TILE_COLS], U8, align_bytes=64)
+                w_codes[(block, kind)] = codes
+                w_scales[(block, kind)] = scales
+                banks[(block, kind)] = []
+                for b in range(BATCH):
+                    bank = psum.tile([P, TILE_COLS], F32, tag="bank")
+                    banks[(block, kind)].append(bank)
+            codes = w_codes[(block, kind)]
+            scales = w_scales[(block, kind)]
+            nc.vector.quantize_mx(
+                out=codes[:, c, :].bitcast(FP8X4), scales=scales[:, c, :], in_=w_grouped[unit][:]
             )
-            copy(out=target[:, heads], in_=source[:, heads, kind])
+            for b in range(BATCH):
+                nc.tensor.matmul_mx(
+                    out=banks[(block, kind)][b][:],
+                    lhsT=x_codes[:, b, c, :].bitcast(FP8X4),
+                    lhsT_scale=x_scales[:, b, c, :],
+                    rhs=codes[:, c, :].bitcast(FP8X4),
+                    rhs_scale=scales[:, c, :],
+                    start=(c == 0),
+                    stop=(c == PASSES - 1),
+                )
 
         def rotate(bank, q_rows):
             by_head = bank[:].rearrange("p (h d) -> p h d", h=BLOCK_HEADS)
@@ -144,54 +140,86 @@ def tile_multiheadlatentattention_pb_kernel(tc, x, cos, sin, wq, out):
                 op=ADD,
             )
 
-        for block in range(BLOCKS):
-            q_tiles = []
-            for b in range(BATCH):
-                q_rows = q_pool.tile([P, BLOCK_HEADS, D_HEAD], F32)
-                q_tiles.append(q_rows)
+        def empty_bank(block, kind, b):
+            bank = banks[(block, kind)][b]
+            q_rows = q_tiles[block][b]
+            if kind == ROPE:
+                rotate(bank, q_rows)
+            else:
+                nc.scalar.copy(
+                    out=q_rows[:, :, :D_CONTENT],
+                    in_=bank[:].rearrange("p (h d) -> p h d", h=BLOCK_HEADS),
+                )
+                heads = slice(block * BLOCK_HEADS, (block + 1) * BLOCK_HEADS)
+                nc.sync.dma_start(out=out[b, :, heads, :], in_=q_rows[:])
 
-            for kind in (ROPE, CONTENT):
-                w_codes = codes_pool.tile([P, PASSES, TILE_COLS], U32, align_bytes=64)
-                w_scales = codes_pool.tile([P, PASSES, TILE_COLS], U8, align_bytes=64)
-                banks = []
-                for b in range(BATCH):
-                    bank = psum.tile([P, TILE_COLS], F32, tag="bank")
-                    banks.append(bank)
+        load_w_chunk(0, 0)
+        x_tiles = []
+        for b in range(BATCH):
+            x_rows = x_pool.tile([P, EMBED], BF16)
+            nc.sync.dma_start(out=x_rows[:], in_=x[b])
+            x_tiles.append(x_rows)
+        for block in range(BLOCKS_AHEAD):
+            for c in range(PASSES):
+                if (block, c) != (0, 0):
+                    load_w_chunk(block, c)
 
-                for c in range(PASSES):
-                    w_grouped = grouped_pool.tile([P, TILE_COLS * PACK], BF16, align_bytes=64)
-                    w_chunk = w_chunks[(block, c)]
-                    regroup(nc.vector.tensor_copy, w_chunk, kind, w_grouped, slice(0, VECTOR_HEADS))
-                    regroup(nc.scalar.copy, w_chunk, kind, w_grouped, slice(VECTOR_HEADS, BLOCK_HEADS))
-                    nc.vector.quantize_mx(
-                        out=w_codes[:, c, :].bitcast(FP8X4),
-                        scales=w_scales[:, c, :],
-                        in_=w_grouped[:],
-                    )
+        cos_rows = const.tile([P, PAIRS], BF16)
+        nc.scalar.dma_start(out=cos_rows[:], in_=cos)
+        sin_rows = const.tile([P, PAIRS], BF16)
+        nc.scalar.dma_start(out=sin_rows[:], in_=sin)
+
+        cos_pairs = const.tile([P, PAIRS, 2], F32)
+        nc.vector.tensor_copy(
+            out=cos_pairs[:], in_=cos_rows[:].unsqueeze(2).to_broadcast([P, PAIRS, 2])
+        )
+        sin_signed = const.tile([P, 2, PAIRS], F32)
+        nc.vector.tensor_scalar_mul(out=sin_signed[:, 0, :], in0=sin_rows[:], scalar1=-1.0)
+        nc.vector.tensor_copy(out=sin_signed[:, 1, :], in_=sin_rows[:])
+
+        identity = const.tile([P, P], F32)
+        make_identity(nc, identity[:])
+
+        regroup(units[0])
+
+        x_codes = const.tile([P, BATCH, PASSES, SEQ], U32, align_bytes=64)
+        x_scales = const.tile([P, BATCH, PASSES, SEQ], U8, align_bytes=64)
+        for b in range(BATCH):
+            x_words = x_tiles[b][:].bitcast(F32).rearrange("r (c q u) -> r c u q", c=PASSES, u=2)
+            x_grouped = x_pool.tile([P, EMBED], BF16, bufs=2, align_bytes=64)
+            grouped_words = x_grouped[:].bitcast(F32).rearrange(
+                "p (c r u) -> p c r u", c=PASSES, u=2
+            )
+            for first, copy in ((0, nc.scalar.copy), (2, nc.vector.tensor_copy)):
+                flipped = psum.tile([P, 2, 2, SEQ], F32, tag="bank")
+                for c in range(2):
+                    for u in range(2):
+                        nc.tensor.transpose(
+                            flipped[:, c, u, :], x_words[:, first + c, u, :], identity[:]
+                        )
+                copy(
+                    out=grouped_words[:, first : first + 2],
+                    in_=flipped[:].rearrange("p c u r -> p c r u"),
+                )
+            nc.vector.quantize_mx(
+                out=x_codes[:, b].rearrange("p c r -> p (c r)").bitcast(FP8X4),
+                scales=x_scales[:, b].rearrange("p c r -> p (c r)"),
+                in_=x_grouped[:],
+            )
+
+        for unit in units[1:REGROUP_AHEAD]:
+            regroup(unit)
+        for step in range(len(units) + PASSES):
+            if step + REGROUP_AHEAD < len(units):
+                regroup(units[step + REGROUP_AHEAD])
+            if step < len(units):
+                block, kind, c = units[step]
+                if kind == ROPE and c == 0:
+                    q_tiles[block] = []
                     for b in range(BATCH):
-                        nc.tensor.matmul_mx(
-                            out=banks[b][:],
-                            lhsT=x_codes[:, b, c, :].bitcast(FP8X4),
-                            lhsT_scale=x_scales[:, b, c, :],
-                            rhs=w_codes[:, c, :].bitcast(FP8X4),
-                            rhs_scale=w_scales[:, c, :],
-                            start=(c == 0),
-                            stop=(c == PASSES - 1),
-                        )
-
-                for b in range(BATCH):
-                    if kind == ROPE:
-                        rotate(banks[b], q_tiles[b])
-                    else:
-                        nc.scalar.copy(
-                            out=q_tiles[b][:, :, :D_CONTENT],
-                            in_=banks[b][:].rearrange("p (h d) -> p h d", h=BLOCK_HEADS),
-                        )
-
-            heads = slice(block * BLOCK_HEADS, (block + 1) * BLOCK_HEADS)
-            for b in range(BATCH):
-                nc.sync.dma_start(out=out[b, :, heads, :], in_=q_tiles[b][:])
-
-            if block + BLOCKS_AHEAD < BLOCKS:
-                for c in range(PASSES):
-                    w_chunks[(block + BLOCKS_AHEAD, c)] = load_w_chunk(block + BLOCKS_AHEAD, c)
+                        q_rows = q_pool.tile([P, BLOCK_HEADS, D_HEAD], F32)
+                        q_tiles[block].append(q_rows)
+                quantise_and_multiply(units[step])
+            if step >= PASSES:
+                block, kind, b = units[step - PASSES]
+                empty_bank(block, kind, b)

@@ -28,7 +28,7 @@ TILE_COLS = BLOCK_HEADS * D_ROPE
 CONTENT, ROPE = 0, 1
 RUN = 4
 
-VECTOR_HEADS = 1
+VECTOR_HEADS = {ROPE: 1, CONTENT: 2}
 REGROUP_AHEAD = 3
 BLOCKS_AHEAD = 3
 
@@ -79,8 +79,9 @@ def tile_multiheadlatentattention_pb_kernel(tc, x, cos, sin, wq, out):
                 "p j (h kind g i) -> p h kind g j i", h=BLOCK_HEADS, kind=2, i=RUN
             )
             target = grouped[:].rearrange("p (h g i j) -> p h g j i", h=BLOCK_HEADS, i=RUN, j=PACK)
-            nc.vector.tensor_copy(out=target[:, :VECTOR_HEADS], in_=source[:, :VECTOR_HEADS, kind])
-            nc.scalar.copy(out=target[:, VECTOR_HEADS:], in_=source[:, VECTOR_HEADS:, kind])
+            split = VECTOR_HEADS[kind]
+            nc.vector.tensor_copy(out=target[:, :split], in_=source[:, :split, kind])
+            nc.scalar.copy(out=target[:, split:], in_=source[:, split:, kind])
             w_grouped[unit] = grouped
             if kind == CONTENT and block + BLOCKS_AHEAD < BLOCKS:
                 load_w_chunk(block + BLOCKS_AHEAD, c)
@@ -133,7 +134,7 @@ def tile_multiheadlatentattention_pb_kernel(tc, x, cos, sin, wq, out):
                     in1=sin_signed[:, two, :].unsqueeze(1).to_broadcast([P, BLOCK_HEADS, PAIRS]),
                     op=MULT,
                 )
-            nc.vector.tensor_tensor(
+            nc.gpsimd.tensor_tensor(
                 out=q_rows[:, :, D_CONTENT:].rearrange("p h (j two) -> p h j two", two=2),
                 in0=cos_term[:],
                 in1=sin_term[:].rearrange("p two h j -> p h j two"),

@@ -28,9 +28,12 @@ TILE_COLS = BLOCK_HEADS * D_ROPE
 CONTENT, ROPE = 0, 1
 RUN = 4
 
-VECTOR_HEADS = {ROPE: 1, CONTENT: 2}
+GROUPS = D_ROPE // RUN
+VECTOR_GROUPS = {(False, False): 16, (True, False): 4, (False, True): 16, (True, True): 8}
 REGROUP_AHEAD = 3
 BLOCKS_AHEAD = 3
+PASS_MAJOR_BLOCKS = 2
+HEAD_UNITS = 2
 
 FLOPS = 2 * BATCH * SEQ * EMBED * HEADS * D_HEAD
 
@@ -41,12 +44,22 @@ def tile_multiheadlatentattention_pb_kernel(tc, x, cos, sin, wq, out):
     nc = tc.nc
     wq_rows = wq.rearrange("(c p j) n -> c p j n", p=P, j=PACK)
 
-    units = [
-        (block, kind, c)
-        for block in range(BLOCKS)
-        for kind in (ROPE, CONTENT)
-        for c in range(PASSES)
-    ]
+    units = []
+    for block in range(BLOCKS):
+        if block < PASS_MAJOR_BLOCKS:
+            units.extend([(block, kind, c) for c in range(PASSES) for kind in (ROPE, CONTENT)])
+        else:
+            units.extend([(block, kind, c) for kind in (ROPE, CONTENT) for c in range(PASSES)])
+
+    due = {}
+    for block in range(BLOCKS):
+        for kind in (ROPE, CONTENT):
+            first = units.index((block, kind, PASSES - 1)) + 1
+            if block < PASS_MAJOR_BLOCKS:
+                first = units.index((block, CONTENT, PASSES - 1)) + 1
+            for b in range(BATCH):
+                due.setdefault(first + b, []).append((block, kind, b))
+    steps = max(due) + 1
 
     with ExitStack() as ctx:
         const = ctx.enter_context(tc.tile_pool(name="const", bufs=1))
@@ -56,7 +69,7 @@ def tile_multiheadlatentattention_pb_kernel(tc, x, cos, sin, wq, out):
         codes_pool = ctx.enter_context(tc.tile_pool(name="codes_pool", bufs=3))
         term_pool = ctx.enter_context(tc.tile_pool(name="term_pool", bufs=3))
         q_pool = ctx.enter_context(tc.tile_pool(name="q_pool", bufs=2 * BATCH))
-        psum = ctx.enter_context(tc.psum_pool(name="psum", bufs=8))
+        psum = ctx.enter_context(tc.psum_pool(name="psum", bufs=1))
         ctx.enter_context(tc.manual_schedule())
 
         w_chunks = {}
@@ -65,6 +78,16 @@ def tile_multiheadlatentattention_pb_kernel(tc, x, cos, sin, wq, out):
         w_scales = {}
         banks = {}
         q_tiles = {}
+        pending = []
+        turn = {}
+        halves = {}
+        for kind in (ROPE, CONTENT):
+            for b in range(BATCH):
+                turn[(kind, b)] = 0
+
+        def bank_tile(kind, b, shape):
+            bank = psum.tile(shape, F32, tag="bank_%d_%d" % (kind, b))
+            return bank
 
         def load_w_chunk(block, c):
             w_chunk = w_pool.tile([P, PACK, BLOCK_COLS], BF16)
@@ -72,46 +95,54 @@ def tile_multiheadlatentattention_pb_kernel(tc, x, cos, sin, wq, out):
             nc.sync.dma_start(out=w_chunk[:], in_=wq_rows[c, :, :, cols])
             w_chunks[(block, c)] = w_chunk
 
-        def regroup(unit):
+        def regroup(unit, step):
             block, kind, c = unit
             grouped = grouped_pool.tile([P, TILE_COLS * PACK], BF16, align_bytes=64)
             source = w_chunks[(block, c)][:].rearrange(
                 "p j (h kind g i) -> p h kind g j i", h=BLOCK_HEADS, kind=2, i=RUN
             )
             target = grouped[:].rearrange("p (h g i j) -> p h g j i", h=BLOCK_HEADS, i=RUN, j=PACK)
-            split = VECTOR_HEADS[kind]
-            nc.vector.tensor_copy(out=target[:, :split], in_=source[:, :split, kind])
-            nc.scalar.copy(out=target[:, split:], in_=source[:, split:, kind])
+            kinds_due = [bank[1] for bank in due.get(step, [])]
+            split = VECTOR_GROUPS[(ROPE in kinds_due, CONTENT in kinds_due)]
+            nc.vector.tensor_copy(out=target[:, :, :split], in_=source[:, :, kind, :split])
+            nc.scalar.copy(out=target[:, :, split:], in_=source[:, :, kind, split:])
             w_grouped[unit] = grouped
             if kind == CONTENT and block + BLOCKS_AHEAD < BLOCKS:
                 load_w_chunk(block + BLOCKS_AHEAD, c)
 
-        def quantise_and_multiply(unit):
+        def quantise(unit):
             block, kind, c = unit
             if c == 0:
                 codes = codes_pool.tile([P, PASSES, TILE_COLS], U32, align_bytes=64)
                 scales = codes_pool.tile([P, PASSES, TILE_COLS], U8, align_bytes=64)
                 w_codes[(block, kind)] = codes
                 w_scales[(block, kind)] = scales
-                banks[(block, kind)] = []
-                for b in range(BATCH):
-                    bank = psum.tile([P, TILE_COLS], F32, tag="bank")
-                    banks[(block, kind)].append(bank)
-            codes = w_codes[(block, kind)]
-            scales = w_scales[(block, kind)]
             nc.vector.quantize_mx(
-                out=codes[:, c, :].bitcast(FP8X4), scales=scales[:, c, :], in_=w_grouped[unit][:]
+                out=w_codes[(block, kind)][:, c, :].bitcast(FP8X4),
+                scales=w_scales[(block, kind)][:, c, :],
+                in_=w_grouped[unit][:],
             )
-            for b in range(BATCH):
+            pending.extend([(block, kind, c, b) for b in range(BATCH)])
+
+        def multiply_what_can_be():
+            waiting = []
+            for block, kind, c, b in pending:
+                if turn[(kind, b)] != block:
+                    waiting.append((block, kind, c, b))
+                    continue
+                if c == 0:
+                    banks[(block, kind, b)] = bank_tile(kind, b, [P, TILE_COLS])
                 nc.tensor.matmul_mx(
-                    out=banks[(block, kind)][b][:],
+                    out=banks[(block, kind, b)][:],
                     lhsT=x_codes[:, b, c, :].bitcast(FP8X4),
                     lhsT_scale=x_scales[:, b, c, :],
-                    rhs=codes[:, c, :].bitcast(FP8X4),
-                    rhs_scale=scales[:, c, :],
+                    rhs=w_codes[(block, kind)][:, c, :].bitcast(FP8X4),
+                    rhs_scale=w_scales[(block, kind)][:, c, :],
                     start=(c == 0),
                     stop=(c == PASSES - 1),
                 )
+            pending.clear()
+            pending.extend(waiting)
 
         def rotate(bank, q_rows):
             by_head = bank[:].rearrange("p (h d) -> p h d", h=BLOCK_HEADS)
@@ -142,15 +173,22 @@ def tile_multiheadlatentattention_pb_kernel(tc, x, cos, sin, wq, out):
             )
 
         def empty_bank(block, kind, b):
-            bank = banks[(block, kind)][b]
-            q_rows = q_tiles[block][b]
+            bank = banks[(block, kind, b)]
+            if (block, b) not in q_tiles:
+                q_rows = q_pool.tile([P, BLOCK_HEADS, D_HEAD], F32)
+                q_tiles[(block, b)] = q_rows
+            q_rows = q_tiles[(block, b)]
             if kind == ROPE:
                 rotate(bank, q_rows)
             else:
-                nc.scalar.copy(
+                copy = nc.vector.tensor_copy if block == BLOCKS - 1 and b % 2 == 1 else nc.scalar.copy
+                copy(
                     out=q_rows[:, :, :D_CONTENT],
                     in_=bank[:].rearrange("p (h d) -> p h d", h=BLOCK_HEADS),
                 )
+            turn[(kind, b)] = block + 1
+            halves[(block, b)] = halves.get((block, b), 0) + 1
+            if halves[(block, b)] == 2:
                 heads = slice(block * BLOCK_HEADS, (block + 1) * BLOCK_HEADS)
                 nc.sync.dma_start(out=out[b, :, heads, :], in_=q_rows[:])
 
@@ -181,7 +219,10 @@ def tile_multiheadlatentattention_pb_kernel(tc, x, cos, sin, wq, out):
         identity = const.tile([P, P], F32)
         make_identity(nc, identity[:])
 
-        regroup(units[0])
+        for unit in units[:HEAD_UNITS]:
+            regroup(unit, -1)
+        for unit in units[:HEAD_UNITS]:
+            quantise(unit)
 
         x_codes = const.tile([P, BATCH, PASSES, SEQ], U32, align_bytes=64)
         x_scales = const.tile([P, BATCH, PASSES, SEQ], U8, align_bytes=64)
@@ -191,8 +232,8 @@ def tile_multiheadlatentattention_pb_kernel(tc, x, cos, sin, wq, out):
             grouped_words = x_grouped[:].bitcast(F32).rearrange(
                 "p (c r u) -> p c r u", c=PASSES, u=2
             )
-            for first, copy in ((0, nc.scalar.copy), (2, nc.vector.tensor_copy)):
-                flipped = psum.tile([P, 2, 2, SEQ], F32, tag="bank")
+            for first, kind, copy in ((0, ROPE, nc.scalar.copy), (2, CONTENT, nc.vector.tensor_copy)):
+                flipped = bank_tile(kind, b, [P, 2, 2, SEQ])
                 for c in range(2):
                     for u in range(2):
                         nc.tensor.transpose(
@@ -207,20 +248,15 @@ def tile_multiheadlatentattention_pb_kernel(tc, x, cos, sin, wq, out):
                 scales=x_scales[:, b].rearrange("p c r -> p (c r)"),
                 in_=x_grouped[:],
             )
+        multiply_what_can_be()
 
-        for unit in units[1:REGROUP_AHEAD]:
-            regroup(unit)
-        for step in range(len(units) + PASSES):
+        for unit in units[HEAD_UNITS : HEAD_UNITS + REGROUP_AHEAD]:
+            regroup(unit, -1)
+        for step in range(HEAD_UNITS, steps):
             if step + REGROUP_AHEAD < len(units):
-                regroup(units[step + REGROUP_AHEAD])
+                regroup(units[step + REGROUP_AHEAD], step)
             if step < len(units):
-                block, kind, c = units[step]
-                if kind == ROPE and c == 0:
-                    q_tiles[block] = []
-                    for b in range(BATCH):
-                        q_rows = q_pool.tile([P, BLOCK_HEADS, D_HEAD], F32)
-                        q_tiles[block].append(q_rows)
-                quantise_and_multiply(units[step])
-            if step >= PASSES:
-                block, kind, b = units[step - PASSES]
+                quantise(units[step])
+            for block, kind, b in due.get(step, []):
                 empty_bank(block, kind, b)
+            multiply_what_can_be()

@@ -24,7 +24,7 @@ PASSES = EMBED // K_PASS
 BLOCK_HEADS = 4
 BLOCK_COLS = BLOCK_HEADS * D_HEAD
 BLOCKS = HEADS // BLOCK_HEADS
-TILE_COLS = BLOCK_HEADS * D_ROPE
+BANK_COLS = 512
 CONTENT, ROPE = 0, 1
 RUN = 4
 
@@ -34,10 +34,11 @@ REGROUP_AHEAD = 3
 BLOCKS_AHEAD = 3
 PASS_MAJOR_BLOCKS = 2
 HEAD_UNITS = 2
+PIECES = ((4,), (4,), (4,), (2, 2))
 
 FLOPS = 2 * BATCH * SEQ * EMBED * HEADS * D_HEAD
 
-assert BATCH == PASSES
+assert BLOCK_HEADS * D_ROPE == BANK_COLS
 
 
 def tile_multiheadlatentattention_pb_kernel(tc, x, cos, sin, wq, out):
@@ -46,20 +47,21 @@ def tile_multiheadlatentattention_pb_kernel(tc, x, cos, sin, wq, out):
 
     units = []
     for block in range(BLOCKS):
+        tiles = []
+        first_head = 0
+        for heads in PIECES[block]:
+            tiles.extend([(block, kind, first_head, heads) for kind in (ROPE, CONTENT)])
+            first_head += heads
         if block < PASS_MAJOR_BLOCKS:
-            units.extend([(block, kind, c) for c in range(PASSES) for kind in (ROPE, CONTENT)])
+            units.extend([(tile, c) for c in range(PASSES) for tile in tiles])
         else:
-            units.extend([(block, kind, c) for kind in (ROPE, CONTENT) for c in range(PASSES)])
-
-    due = {}
-    for block in range(BLOCKS):
-        for kind in (ROPE, CONTENT):
-            first = units.index((block, kind, PASSES - 1)) + 1
-            if block < PASS_MAJOR_BLOCKS:
-                first = units.index((block, CONTENT, PASSES - 1)) + 1
-            for b in range(BATCH):
-                due.setdefault(first + b, []).append((block, kind, b))
-    steps = max(due) + 1
+            units.extend([(tile, c) for tile in tiles for c in range(PASSES)])
+    bank_users = {ROPE: [], CONTENT: []}
+    last_reader = {}
+    for tile, c in units:
+        if c == 0:
+            bank_users[tile[1]].append(tile)
+        last_reader[(tile[0], c)] = (tile, c)
 
     with ExitStack() as ctx:
         const = ctx.enter_context(tc.tile_pool(name="const", bufs=1))
@@ -80,6 +82,8 @@ def tile_multiheadlatentattention_pb_kernel(tc, x, cos, sin, wq, out):
         q_tiles = {}
         pending = []
         turn = {}
+        full = {}
+        emptied = set()
         halves = {}
         for kind in (ROPE, CONTENT):
             for b in range(BATCH):
@@ -95,102 +99,118 @@ def tile_multiheadlatentattention_pb_kernel(tc, x, cos, sin, wq, out):
             nc.sync.dma_start(out=w_chunk[:], in_=wq_rows[c, :, :, cols])
             w_chunks[(block, c)] = w_chunk
 
-        def regroup(unit, step):
-            block, kind, c = unit
-            grouped = grouped_pool.tile([P, TILE_COLS * PACK], BF16, align_bytes=64)
+        def regroup(unit, kinds_due):
+            (block, kind, first_head, heads), c = unit
+            grouped = grouped_pool.tile([P, heads * D_ROPE * PACK], BF16, align_bytes=64)
             source = w_chunks[(block, c)][:].rearrange(
                 "p j (h kind g i) -> p h kind g j i", h=BLOCK_HEADS, kind=2, i=RUN
-            )
-            target = grouped[:].rearrange("p (h g i j) -> p h g j i", h=BLOCK_HEADS, i=RUN, j=PACK)
-            kinds_due = [bank[1] for bank in due.get(step, [])]
+            )[:, first_head : first_head + heads, kind]
+            target = grouped[:].rearrange("p (h g i j) -> p h g j i", h=heads, i=RUN, j=PACK)
             split = VECTOR_GROUPS[(ROPE in kinds_due, CONTENT in kinds_due)]
-            nc.vector.tensor_copy(out=target[:, :, :split], in_=source[:, :, kind, :split])
-            nc.scalar.copy(out=target[:, :, split:], in_=source[:, :, kind, split:])
+            nc.vector.tensor_copy(out=target[:, :, :split], in_=source[:, :, :split])
+            nc.scalar.copy(out=target[:, :, split:], in_=source[:, :, split:])
             w_grouped[unit] = grouped
-            if kind == CONTENT and block + BLOCKS_AHEAD < BLOCKS:
+            if last_reader[(block, c)] == unit and block + BLOCKS_AHEAD < BLOCKS:
                 load_w_chunk(block + BLOCKS_AHEAD, c)
 
         def quantise(unit):
-            block, kind, c = unit
+            tile, c = unit
+            cols = tile[3] * D_ROPE
             if c == 0:
-                codes = codes_pool.tile([P, PASSES, TILE_COLS], U32, align_bytes=64)
-                scales = codes_pool.tile([P, PASSES, TILE_COLS], U8, align_bytes=64)
-                w_codes[(block, kind)] = codes
-                w_scales[(block, kind)] = scales
+                codes = codes_pool.tile([P, PASSES, cols], U32, align_bytes=64)
+                scales = codes_pool.tile([P, PASSES, cols], U8, align_bytes=64)
+                w_codes[tile] = codes
+                w_scales[tile] = scales
             nc.vector.quantize_mx(
-                out=w_codes[(block, kind)][:, c, :].bitcast(FP8X4),
-                scales=w_scales[(block, kind)][:, c, :],
+                out=w_codes[tile][:, c, :].bitcast(FP8X4),
+                scales=w_scales[tile][:, c, :],
                 in_=w_grouped[unit][:],
             )
-            pending.extend([(block, kind, c, b) for b in range(BATCH)])
+            pending.extend([(tile, c, b) for b in range(BATCH)])
 
-        def multiply_what_can_be():
+        def multiply_what_can_be(step):
             waiting = []
-            for block, kind, c, b in pending:
-                if turn[(kind, b)] != block:
-                    waiting.append((block, kind, c, b))
+            for tile, c, b in pending:
+                kind = tile[1]
+                if bank_users[kind][turn[(kind, b)]] != tile:
+                    waiting.append((tile, c, b))
                     continue
                 if c == 0:
-                    banks[(block, kind, b)] = bank_tile(kind, b, [P, TILE_COLS])
+                    banks[(tile, b)] = bank_tile(kind, b, [P, tile[3] * D_ROPE])
                 nc.tensor.matmul_mx(
-                    out=banks[(block, kind, b)][:],
+                    out=banks[(tile, b)][:],
                     lhsT=x_codes[:, b, c, :].bitcast(FP8X4),
                     lhsT_scale=x_scales[:, b, c, :],
-                    rhs=w_codes[(block, kind)][:, c, :].bitcast(FP8X4),
-                    rhs_scale=w_scales[(block, kind)][:, c, :],
+                    rhs=w_codes[tile][:, c, :].bitcast(FP8X4),
+                    rhs_scale=w_scales[tile][:, c, :],
                     start=(c == 0),
                     stop=(c == PASSES - 1),
                 )
+                if c == PASSES - 1:
+                    full[(tile, b)] = step
             pending.clear()
             pending.extend(waiting)
 
-        def rotate(bank, q_rows):
-            by_head = bank[:].rearrange("p (h d) -> p h d", h=BLOCK_HEADS)
-            by_pair = bank[:].rearrange("p (h j two) -> p h j two", h=BLOCK_HEADS, two=2)
-            cos_term = term_pool.tile([P, BLOCK_HEADS, PAIRS, 2], F32)
+        def rotate(bank, q_part, heads):
+            by_head = bank[:].rearrange("p (h d) -> p h d", h=heads)
+            by_pair = bank[:].rearrange("p (h j two) -> p h j two", h=heads, two=2)
+            cos_term = term_pool.tile([P, heads, PAIRS, 2], F32)
             nc.vector.tensor_tensor(
                 out=cos_term[:].rearrange("p h j two -> p h (j two)"),
                 in0=by_head,
                 in1=cos_pairs[:]
                 .rearrange("p j two -> p (j two)")
                 .unsqueeze(1)
-                .to_broadcast([P, BLOCK_HEADS, D_ROPE]),
+                .to_broadcast([P, heads, D_ROPE]),
                 op=MULT,
             )
-            sin_term = term_pool.tile([P, 2, BLOCK_HEADS, PAIRS], F32)
+            sin_term = term_pool.tile([P, 2, heads, PAIRS], F32)
             for two in range(2):
                 nc.vector.tensor_tensor(
                     out=sin_term[:, two],
                     in0=by_pair[:, :, :, 1 - two],
-                    in1=sin_signed[:, two, :].unsqueeze(1).to_broadcast([P, BLOCK_HEADS, PAIRS]),
+                    in1=sin_signed[:, two, :].unsqueeze(1).to_broadcast([P, heads, PAIRS]),
                     op=MULT,
                 )
             nc.gpsimd.tensor_tensor(
-                out=q_rows[:, :, D_CONTENT:].rearrange("p h (j two) -> p h j two", two=2),
+                out=q_part.rearrange("p h (j two) -> p h j two", two=2),
                 in0=cos_term[:],
                 in1=sin_term[:].rearrange("p two h j -> p h j two"),
                 op=ADD,
             )
 
-        def empty_bank(block, kind, b):
-            bank = banks[(block, kind, b)]
+        def empty_bank(tile, b, copy):
+            block, kind, first_head, heads = tile
+            bank = banks[(tile, b)]
             if (block, b) not in q_tiles:
                 q_rows = q_pool.tile([P, BLOCK_HEADS, D_HEAD], F32)
                 q_tiles[(block, b)] = q_rows
-            q_rows = q_tiles[(block, b)]
+            q_piece = q_tiles[(block, b)][:, first_head : first_head + heads, :]
             if kind == ROPE:
-                rotate(bank, q_rows)
+                rotate(bank, q_piece[:, :, D_CONTENT:], heads)
             else:
-                copy = nc.vector.tensor_copy if block == BLOCKS - 1 and b % 2 == 1 else nc.scalar.copy
-                copy(
-                    out=q_rows[:, :, :D_CONTENT],
-                    in_=bank[:].rearrange("p (h d) -> p h d", h=BLOCK_HEADS),
+                copy(out=q_piece[:, :, :D_CONTENT], in_=bank[:].rearrange("p (h d) -> p h d", h=heads))
+            turn[(kind, b)] += 1
+            piece = (block, first_head, b)
+            halves[piece] = halves.get(piece, 0) + 1
+            if halves[piece] == 2:
+                head = block * BLOCK_HEADS + first_head
+                nc.sync.dma_start(out=out[b, :, head : head + heads, :], in_=q_piece)
+
+        def banks_due(step):
+            chosen = []
+            for kind in (ROPE, CONTENT):
+                ready = sorted(
+                    [
+                        (full[(tile, b)], bank_users[kind].index(tile), b)
+                        for tile, b in full
+                        if tile[1] == kind and full[(tile, b)] < step and (tile, b) not in emptied
+                    ]
                 )
-            turn[(kind, b)] = block + 1
-            halves[(block, b)] = halves.get((block, b), 0) + 1
-            if halves[(block, b)] == 2:
-                heads = slice(block * BLOCK_HEADS, (block + 1) * BLOCK_HEADS)
-                nc.sync.dma_start(out=out[b, :, heads, :], in_=q_rows[:])
+                if step < len(units):
+                    ready = ready[:1]
+                chosen.extend([(bank_users[kind][index], b) for since, index, b in ready])
+            return chosen
 
         load_w_chunk(0, 0)
         x_tiles = []
@@ -220,7 +240,7 @@ def tile_multiheadlatentattention_pb_kernel(tc, x, cos, sin, wq, out):
         make_identity(nc, identity[:])
 
         for unit in units[:HEAD_UNITS]:
-            regroup(unit, -1)
+            regroup(unit, [])
         for unit in units[:HEAD_UNITS]:
             quantise(unit)
 
@@ -248,15 +268,22 @@ def tile_multiheadlatentattention_pb_kernel(tc, x, cos, sin, wq, out):
                 scales=x_scales[:, b].rearrange("p c r -> p (c r)"),
                 in_=x_grouped[:],
             )
-        multiply_what_can_be()
+        multiply_what_can_be(0)
 
         for unit in units[HEAD_UNITS : HEAD_UNITS + REGROUP_AHEAD]:
-            regroup(unit, -1)
-        for step in range(HEAD_UNITS, steps):
+            regroup(unit, [])
+        for step in range(HEAD_UNITS, len(units) + 1):
+            due = banks_due(step)
             if step + REGROUP_AHEAD < len(units):
-                regroup(units[step + REGROUP_AHEAD], step)
+                regroup(units[step + REGROUP_AHEAD], [tile[1] for tile, b in due])
             if step < len(units):
                 quantise(units[step])
-            for block, kind, b in due.get(step, []):
-                empty_bank(block, kind, b)
-            multiply_what_can_be()
+            content_banks = 0
+            for tile, b in due:
+                by_vector = step >= len(units) and content_banks % 2 == 1
+                empty_bank(tile, b, nc.vector.tensor_copy if by_vector else nc.scalar.copy)
+                emptied.add((tile, b))
+                if tile[1] == CONTENT:
+                    content_banks += 1
+            multiply_what_can_be(step)
+        assert not pending and len(emptied) == len(full)

@@ -34,6 +34,7 @@ REGROUP_AHEAD = 3
 BLOCKS_AHEAD = 3
 PASS_MAJOR_BLOCKS = 2
 HEAD_UNITS = 2
+EMPTY_AFTER = {ROPE: 2, CONTENT: 1}
 PIECES = ((4,), (4,), (4,), (2, 2))
 
 FLOPS = 2 * BATCH * SEQ * EMBED * HEADS * D_HEAD
@@ -204,7 +205,9 @@ def tile_multiheadlatentattention_pb_kernel(tc, x, cos, sin, wq, out):
                     [
                         (full[(tile, b)], bank_users[kind].index(tile), b)
                         for tile, b in full
-                        if tile[1] == kind and full[(tile, b)] < step and (tile, b) not in emptied
+                        if tile[1] == kind
+                        and full[(tile, b)] + EMPTY_AFTER[kind] <= step
+                        and (tile, b) not in emptied
                     ]
                 )
                 if step < len(units):
@@ -272,7 +275,7 @@ def tile_multiheadlatentattention_pb_kernel(tc, x, cos, sin, wq, out):
 
         for unit in units[HEAD_UNITS : HEAD_UNITS + REGROUP_AHEAD]:
             regroup(unit, [])
-        for step in range(HEAD_UNITS, len(units) + 1):
+        for step in range(HEAD_UNITS, len(units) + max(EMPTY_AFTER[ROPE], EMPTY_AFTER[CONTENT])):
             due = banks_due(step)
             if step + REGROUP_AHEAD < len(units):
                 regroup(units[step + REGROUP_AHEAD], [tile[1] for tile, b in due])

@@ -29,8 +29,8 @@ CONTENT, ROPE = 0, 1
 RUN = 4
 
 GROUPS = D_ROPE // RUN
-VECTOR_GROUPS = {(False, False): 16, (True, False): 4, (False, True): 16, (True, True): 8}
-REGROUP_AHEAD = 3
+VECTOR_GROUPS = {(False, False): 14, (True, False): 4, (False, True): 18, (True, True): 10}
+REGROUP_AHEAD = 2
 BLOCKS_AHEAD = 3
 PASS_MAJOR_BLOCKS = 2
 HEAD_UNITS = 2

@@ -153,30 +153,27 @@ def tile_multiheadlatentattention_pb_kernel(tc, x, cos, sin, wq, out):
             pending.extend(waiting)
 
         def rotate(bank, q_part, heads):
-            by_head = bank[:].rearrange("p (h d) -> p h d", h=heads)
-            by_pair = bank[:].rearrange("p (h j two) -> p h j two", h=heads, two=2)
-            cos_term = term_pool.tile([P, heads, PAIRS, 2], F32)
+            cos_term = term_pool.tile([P, heads, D_ROPE], F32)
             nc.vector.tensor_tensor(
-                out=cos_term[:].rearrange("p h j two -> p h (j two)"),
-                in0=by_head,
+                out=cos_term[:],
+                in0=bank[:].rearrange("p (h d) -> p h d", h=heads),
                 in1=cos_pairs[:]
                 .rearrange("p j two -> p (j two)")
                 .unsqueeze(1)
                 .to_broadcast([P, heads, D_ROPE]),
                 op=MULT,
             )
-            sin_term = term_pool.tile([P, 2, heads, PAIRS], F32)
-            for two in range(2):
-                nc.vector.tensor_tensor(
-                    out=sin_term[:, two],
-                    in0=by_pair[:, :, :, 1 - two],
-                    in1=sin_signed[:, two, :].unsqueeze(1).to_broadcast([P, heads, PAIRS]),
-                    op=MULT,
-                )
+            sin_term = term_pool.tile([P, heads, PAIRS, 2], F32)
+            nc.vector.tensor_tensor(
+                out=sin_term[:],
+                in0=bank[:].rearrange("p (h j two) -> p h j two", h=heads, two=2)[:, :, :, ::-1],
+                in1=sin_signed[:].unsqueeze(1).to_broadcast([P, heads, PAIRS, 2]),
+                op=MULT,
+            )
             nc.gpsimd.tensor_tensor(
-                out=q_part.rearrange("p h (j two) -> p h j two", two=2),
+                out=q_part,
                 in0=cos_term[:],
-                in1=sin_term[:].rearrange("p two h j -> p h j two"),
+                in1=sin_term[:].rearrange("p h j two -> p h (j two)"),
                 op=ADD,
             )
 
@@ -235,9 +232,9 @@ def tile_multiheadlatentattention_pb_kernel(tc, x, cos, sin, wq, out):
         nc.vector.tensor_copy(
             out=cos_pairs[:], in_=cos_rows[:].unsqueeze(2).to_broadcast([P, PAIRS, 2])
         )
-        sin_signed = const.tile([P, 2, PAIRS], F32)
-        nc.vector.tensor_scalar_mul(out=sin_signed[:, 0, :], in0=sin_rows[:], scalar1=-1.0)
-        nc.vector.tensor_copy(out=sin_signed[:, 1, :], in_=sin_rows[:])
+        sin_signed = const.tile([P, PAIRS, 2], F32)
+        nc.vector.tensor_scalar_mul(out=sin_signed[:, :, 0], in0=sin_rows[:], scalar1=-1.0)
+        nc.vector.tensor_copy(out=sin_signed[:, :, 1], in_=sin_rows[:])
 
         identity = const.tile([P, P], F32)
         make_identity(nc, identity[:])

@@ -156,18 +156,18 @@ def tile_multiheadlatentattention_pb_kernel(tc, x, cos, sin, wq, out):
             cos_term = term_pool.tile([P, heads, D_ROPE], F32)
             nc.vector.tensor_tensor(
                 out=cos_term[:],
-                in0=bank[:].rearrange("p (h d) -> p h d", h=heads),
-                in1=cos_pairs[:]
+                in0=cos_pairs[:]
                 .rearrange("p j two -> p (j two)")
                 .unsqueeze(1)
                 .to_broadcast([P, heads, D_ROPE]),
+                in1=bank[:].rearrange("p (h d) -> p h d", h=heads),
                 op=MULT,
             )
             sin_term = term_pool.tile([P, heads, PAIRS, 2], F32)
             nc.vector.tensor_tensor(
                 out=sin_term[:],
-                in0=bank[:].rearrange("p (h j two) -> p h j two", h=heads, two=2)[:, :, :, ::-1],
-                in1=sin_signed[:].unsqueeze(1).to_broadcast([P, heads, PAIRS, 2]),
+                in0=sin_signed[:].unsqueeze(1).to_broadcast([P, heads, PAIRS, 2]),
+                in1=bank[:].rearrange("p (h j two) -> p h j two", h=heads, two=2)[:, :, :, ::-1],
                 op=MULT,
             )
             nc.gpsimd.tensor_tensor(

@@ -153,27 +153,20 @@ def tile_multiheadlatentattention_pb_kernel(tc, x, cos, sin, wq, out):
             pending.extend(waiting)
 
         def rotate(bank, q_part, heads):
-            cos_term = term_pool.tile([P, heads, D_ROPE], F32)
+            terms = term_pool.tile([P, 2, heads, D_ROPE], F32)
             nc.vector.tensor_tensor(
-                out=cos_term[:],
-                in0=cos_pairs[:]
-                .rearrange("p j two -> p (j two)")
+                out=terms[:],
+                in0=tables[:].unsqueeze(2).to_broadcast([P, 2, heads, D_ROPE]),
+                in1=bank[:]
+                .rearrange("p (h d) -> p h d", h=heads)
                 .unsqueeze(1)
-                .to_broadcast([P, heads, D_ROPE]),
-                in1=bank[:].rearrange("p (h d) -> p h d", h=heads),
-                op=MULT,
-            )
-            sin_term = term_pool.tile([P, heads, PAIRS, 2], F32)
-            nc.vector.tensor_tensor(
-                out=sin_term[:],
-                in0=sin_signed[:].unsqueeze(1).to_broadcast([P, heads, PAIRS, 2]),
-                in1=bank[:].rearrange("p (h j two) -> p h j two", h=heads, two=2)[:, :, :, ::-1],
+                .to_broadcast([P, 2, heads, D_ROPE]),
                 op=MULT,
             )
             nc.gpsimd.tensor_tensor(
-                out=q_part,
-                in0=cos_term[:],
-                in1=sin_term[:].rearrange("p h j two -> p h (j two)"),
+                out=q_part.rearrange("p h (j two) -> p h j two", two=2),
+                in0=terms[:, 0].rearrange("p h (j two) -> p h j two", two=2),
+                in1=terms[:, 1].rearrange("p h (j two) -> p h j two", two=2)[:, :, :, ::-1],
                 op=ADD,
             )
 
@@ -228,13 +221,14 @@ def tile_multiheadlatentattention_pb_kernel(tc, x, cos, sin, wq, out):
         sin_rows = const.tile([P, PAIRS], BF16)
         nc.scalar.dma_start(out=sin_rows[:], in_=sin)
 
-        cos_pairs = const.tile([P, PAIRS, 2], F32)
+        tables = const.tile([P, 2, D_ROPE], F32)
         nc.vector.tensor_copy(
-            out=cos_pairs[:], in_=cos_rows[:].unsqueeze(2).to_broadcast([P, PAIRS, 2])
+            out=tables[:, 0].rearrange("p (j two) -> p j two", two=2),
+            in_=cos_rows[:].unsqueeze(2).to_broadcast([P, PAIRS, 2]),
         )
-        sin_signed = const.tile([P, PAIRS, 2], F32)
-        nc.vector.tensor_scalar_mul(out=sin_signed[:, :, 0], in0=sin_rows[:], scalar1=-1.0)
-        nc.vector.tensor_copy(out=sin_signed[:, :, 1], in_=sin_rows[:])
+        sin_pairs = tables[:, 1].rearrange("p (j two) -> p j two", two=2)
+        nc.vector.tensor_copy(out=sin_pairs[:, :, 0], in_=sin_rows[:])
+        nc.vector.tensor_scalar_mul(out=sin_pairs[:, :, 1], in0=sin_rows[:], scalar1=-1.0)
 
         identity = const.tile([P, P], F32)
         make_identity(nc, identity[:])

@@ -30,6 +30,8 @@ RUN = 4
 
 GROUPS = D_ROPE // RUN
 VECTOR_GROUPS = {(False, False): 14, (True, False): 4, (False, True): 18, (True, True): 10}
+EARLY_UNITS = 8
+EARLY_GROUPS = 16
 REGROUP_AHEAD = 2
 BLOCKS_AHEAD = 3
 PASS_MAJOR_BLOCKS = 2
@@ -108,6 +110,8 @@ def tile_multiheadlatentattention_pb_kernel(tc, x, cos, sin, wq, out):
             )[:, first_head : first_head + heads, kind]
             target = grouped[:].rearrange("p (h g i j) -> p h g j i", h=heads, i=RUN, j=PACK)
             split = VECTOR_GROUPS[(ROPE in kinds_due, CONTENT in kinds_due)]
+            if units.index(unit) < EARLY_UNITS:
+                split = EARLY_GROUPS
             nc.vector.tensor_copy(out=target[:, :, :split], in_=source[:, :, :split])
             nc.scalar.copy(out=target[:, :, split:], in_=source[:, :, split:])
             w_grouped[unit] = grouped
@@ -246,14 +250,14 @@ def tile_multiheadlatentattention_pb_kernel(tc, x, cos, sin, wq, out):
             grouped_words = x_grouped[:].bitcast(F32).rearrange(
                 "p (c r u) -> p c r u", c=PASSES, u=2
             )
-            for first, kind, copy in ((0, ROPE, nc.scalar.copy), (2, CONTENT, nc.vector.tensor_copy)):
+            for first, kind in ((0, ROPE), (2, CONTENT)):
                 flipped = bank_tile(kind, b, [P, 2, 2, SEQ])
                 for c in range(2):
                     for u in range(2):
                         nc.tensor.transpose(
                             flipped[:, c, u, :], x_words[:, first + c, u, :], identity[:]
                         )
-                copy(
+                nc.scalar.copy(
                     out=grouped_words[:, first : first + 2],
                     in_=flipped[:].rearrange("p c u r -> p c r u"),
                 )

@@ -72,8 +72,8 @@ def tile_multiheadlatentattention_pb_kernel(tc, x, cos, sin, wq, out):
         w_pool = ctx.enter_context(tc.tile_pool(name="w_pool", bufs=BLOCKS_AHEAD * PASSES))
         grouped_pool = ctx.enter_context(tc.tile_pool(name="grouped_pool", bufs=REGROUP_AHEAD + 2))
         codes_pool = ctx.enter_context(tc.tile_pool(name="codes_pool", bufs=3))
-        term_pool = ctx.enter_context(tc.tile_pool(name="term_pool", bufs=3))
-        q_pool = ctx.enter_context(tc.tile_pool(name="q_pool", bufs=2 * BATCH))
+        term_pool = ctx.enter_context(tc.tile_pool(name="term_pool", bufs=4))
+        q_pool = ctx.enter_context(tc.tile_pool(name="q_pool", bufs=10))
         psum = ctx.enter_context(tc.psum_pool(name="psum", bufs=1))
         ctx.enter_context(tc.manual_schedule())
 

from contextlib import ExitStack

import concourse.mybir as mybir
from concourse.masks import make_identity

F32 = mybir.dt.float32
BF16 = mybir.dt.bfloat16
U32 = mybir.dt.uint32
U8 = mybir.dt.uint8
FP8X4 = mybir.dt.float8_e4m3fn_x4
MULT = mybir.AluOpType.mult
ADD = mybir.AluOpType.add

P = 128
PACK = 4
K_PASS = P * PACK

BATCH, SEQ, EMBED = 4, 128, 2048
HEADS, D_CONTENT, D_ROPE = 16, 128, 128
D_HEAD = D_CONTENT + D_ROPE
PAIRS = D_ROPE // 2
PASSES = EMBED // K_PASS

BLOCK_HEADS = 4
BLOCK_COLS = BLOCK_HEADS * D_HEAD
BLOCKS = HEADS // BLOCK_HEADS
BANK_COLS = 512
CONTENT, ROPE = 0, 1
RUN = 4

GROUPS = D_ROPE // RUN
VECTOR_GROUPS = {(False, False): 14, (True, False): 4, (False, True): 18, (True, True): 10}
EARLY_UNITS = 8
EARLY_GROUPS = 16
REGROUP_AHEAD = 2
BLOCKS_AHEAD = 3
PASS_MAJOR_BLOCKS = 2
HEAD_UNITS = 2
EMPTY_AFTER = {ROPE: 2, CONTENT: 1}
PIECES = ((4,), (4,), (4,), (2, 2))

FLOPS = 2 * BATCH * SEQ * EMBED * HEADS * D_HEAD

assert BLOCK_HEADS * D_ROPE == BANK_COLS


def tile_multiheadlatentattention_pb_kernel(tc, x, cos, sin, wq, out):
    nc = tc.nc
    wq_rows = wq.rearrange("(c p j) n -> c p j n", p=P, j=PACK)

    units = []
    for block in range(BLOCKS):
        tiles = []
        first_head = 0
        for heads in PIECES[block]:
            tiles.extend([(block, kind, first_head, heads) for kind in (ROPE, CONTENT)])
            first_head += heads
        if block < PASS_MAJOR_BLOCKS:
            units.extend([(tile, c) for c in range(PASSES) for tile in tiles])
        else:
            units.extend([(tile, c) for tile in tiles for c in range(PASSES)])
    bank_users = {ROPE: [], CONTENT: []}
    last_reader = {}
    for tile, c in units:
        if c == 0:
            bank_users[tile[1]].append(tile)
        last_reader[(tile[0], c)] = (tile, c)

    with ExitStack() as ctx:
        const = ctx.enter_context(tc.tile_pool(name="const", bufs=1))
        x_pool = ctx.enter_context(tc.tile_pool(name="x_pool", bufs=BATCH))
        w_pool = ctx.enter_context(tc.tile_pool(name="w_pool", bufs=BLOCKS_AHEAD * PASSES))
        grouped_pool = ctx.enter_context(tc.tile_pool(name="grouped_pool", bufs=REGROUP_AHEAD + 2))
        codes_pool = ctx.enter_context(tc.tile_pool(name="codes_pool", bufs=3))
        term_pool = ctx.enter_context(tc.tile_pool(name="term_pool", bufs=4))
        q_pool = ctx.enter_context(tc.tile_pool(name="q_pool", bufs=10))
        psum = ctx.enter_context(tc.psum_pool(name="psum", bufs=1))
        ctx.enter_context(tc.manual_schedule())

        w_chunks = {}
        w_grouped = {}
        w_codes = {}
        w_scales = {}
        banks = {}
        q_tiles = {}
        pending = []
        turn = {}
        full = {}
        emptied = set()
        halves = {}
        for kind in (ROPE, CONTENT):
            for b in range(BATCH):
                turn[(kind, b)] = 0

        def bank_tile(kind, b, shape):
            bank = psum.tile(shape, F32, tag="bank_%d_%d" % (kind, b))
            return bank

        def load_w_chunk(block, c):
            w_chunk = w_pool.tile([P, PACK, BLOCK_COLS], BF16)
            cols = slice(block * BLOCK_COLS, (block + 1) * BLOCK_COLS)
            nc.sync.dma_start(out=w_chunk[:], in_=wq_rows[c, :, :, cols])
            w_chunks[(block, c)] = w_chunk

        def regroup(unit, kinds_due):
            (block, kind, first_head, heads), c = unit
            grouped = grouped_pool.tile([P, heads * D_ROPE * PACK], BF16, align_bytes=64)
            source = w_chunks[(block, c)][:].rearrange(
                "p j (h kind g i) -> p h kind g j i", h=BLOCK_HEADS, kind=2, i=RUN
            )[:, first_head : first_head + heads, kind]
            target = grouped[:].rearrange("p (h g i j) -> p h g j i", h=heads, i=RUN, j=PACK)
            split = VECTOR_GROUPS[(ROPE in kinds_due, CONTENT in kinds_due)]
            if units.index(unit) < EARLY_UNITS:
                split = EARLY_GROUPS
            nc.vector.tensor_copy(out=target[:, :, :split], in_=source[:, :, :split])
            nc.scalar.copy(out=target[:, :, split:], in_=source[:, :, split:])
            w_grouped[unit] = grouped
            if last_reader[(block, c)] == unit and block + BLOCKS_AHEAD < BLOCKS:
                load_w_chunk(block + BLOCKS_AHEAD, c)

        def quantise(unit):
            tile, c = unit
            cols = tile[3] * D_ROPE
            if c == 0:
                codes = codes_pool.tile([P, PASSES, cols], U32, align_bytes=64)
                scales = codes_pool.tile([P, PASSES, cols], U8, align_bytes=64)
                w_codes[tile] = codes
                w_scales[tile] = scales
            nc.vector.quantize_mx(
                out=w_codes[tile][:, c, :].bitcast(FP8X4),
                scales=w_scales[tile][:, c, :],
                in_=w_grouped[unit][:],
            )
            pending.extend([(tile, c, b) for b in range(BATCH)])

        def multiply_what_can_be(step):
            waiting = []
            for tile, c, b in pending:
                kind = tile[1]
                if bank_users[kind][turn[(kind, b)]] != tile:
                    waiting.append((tile, c, b))
                    continue
                if c == 0:
                    banks[(tile, b)] = bank_tile(kind, b, [P, tile[3] * D_ROPE])
                nc.tensor.matmul_mx(
                    out=banks[(tile, b)][:],
                    lhsT=x_codes[:, b, c, :].bitcast(FP8X4),
                    lhsT_scale=x_scales[:, b, c, :],
                    rhs=w_codes[tile][:, c, :].bitcast(FP8X4),
                    rhs_scale=w_scales[tile][:, c, :],
                    start=(c == 0),
                    stop=(c == PASSES - 1),
                )
                if c == PASSES - 1:
                    full[(tile, b)] = step
            pending.clear()
            pending.extend(waiting)

        def rotate(bank, q_part, heads):
            terms = term_pool.tile([P, 2, heads, D_ROPE], F32)
            nc.vector.tensor_tensor(
                out=terms[:],
                in0=tables[:].unsqueeze(2).to_broadcast([P, 2, heads, D_ROPE]),
                in1=bank[:]
                .rearrange("p (h d) -> p h d", h=heads)
                .unsqueeze(1)
                .to_broadcast([P, 2, heads, D_ROPE]),
                op=MULT,
            )
            nc.gpsimd.tensor_tensor(
                out=q_part.rearrange("p h (j two) -> p h j two", two=2),
                in0=terms[:, 0].rearrange("p h (j two) -> p h j two", two=2),
                in1=terms[:, 1].rearrange("p h (j two) -> p h j two", two=2)[:, :, :, ::-1],
                op=ADD,
            )

        def empty_bank(tile, b, copy):
            block, kind, first_head, heads = tile
            bank = banks[(tile, b)]
            if (block, b) not in q_tiles:
                q_rows = q_pool.tile([P, BLOCK_HEADS, D_HEAD], F32)
                q_tiles[(block, b)] = q_rows
            q_piece = q_tiles[(block, b)][:, first_head : first_head + heads, :]
            if kind == ROPE:
                rotate(bank, q_piece[:, :, D_CONTENT:], heads)
            else:
                copy(out=q_piece[:, :, :D_CONTENT], in_=bank[:].rearrange("p (h d) -> p h d", h=heads))
            turn[(kind, b)] += 1
            piece = (block, first_head, b)
            halves[piece] = halves.get(piece, 0) + 1
            if halves[piece] == 2:
                head = block * BLOCK_HEADS + first_head
                nc.sync.dma_start(out=out[b, :, head : head + heads, :], in_=q_piece)

        def banks_due(step):
            chosen = []
            for kind in (ROPE, CONTENT):
                ready = sorted(
                    [
                        (full[(tile, b)], bank_users[kind].index(tile), b)
                        for tile, b in full
                        if tile[1] == kind
                        and full[(tile, b)] + EMPTY_AFTER[kind] <= step
                        and (tile, b) not in emptied
                    ]
                )
                if step < len(units):
                    ready = ready[:1]
                chosen.extend([(bank_users[kind][index], b) for since, index, b in ready])
            return chosen

        load_w_chunk(0, 0)
        x_tiles = []
        for b in range(BATCH):
            x_rows = x_pool.tile([P, EMBED], BF16)
            nc.sync.dma_start(out=x_rows[:], in_=x[b])
            x_tiles.append(x_rows)
        for block in range(BLOCKS_AHEAD):
            for c in range(PASSES):
                if (block, c) != (0, 0):
                    load_w_chunk(block, c)

        cos_rows = const.tile([P, PAIRS], BF16)
        nc.scalar.dma_start(out=cos_rows[:], in_=cos)
        sin_rows = const.tile([P, PAIRS], BF16)
        nc.scalar.dma_start(out=sin_rows[:], in_=sin)

        tables = const.tile([P, 2, D_ROPE], F32)
        nc.vector.tensor_copy(
            out=tables[:, 0].rearrange("p (j two) -> p j two", two=2),
            in_=cos_rows[:].unsqueeze(2).to_broadcast([P, PAIRS, 2]),
        )
        sin_pairs = tables[:, 1].rearrange("p (j two) -> p j two", two=2)
        nc.vector.tensor_copy(out=sin_pairs[:, :, 0], in_=sin_rows[:])
        nc.vector.tensor_scalar_mul(out=sin_pairs[:, :, 1], in0=sin_rows[:], scalar1=-1.0)

        identity = const.tile([P, P], F32)
        make_identity(nc, identity[:])

        for unit in units[:HEAD_UNITS]:
            regroup(unit, [])
        for unit in units[:HEAD_UNITS]:
            quantise(unit)

        x_codes = const.tile([P, BATCH, PASSES, SEQ], U32, align_bytes=64)
        x_scales = const.tile([P, BATCH, PASSES, SEQ], U8, align_bytes=64)
        for b in range(BATCH):
            x_words = x_tiles[b][:].bitcast(F32).rearrange("r (c q u) -> r c u q", c=PASSES, u=2)
            x_grouped = x_pool.tile([P, EMBED], BF16, bufs=2, align_bytes=64)
            grouped_words = x_grouped[:].bitcast(F32).rearrange(
                "p (c r u) -> p c r u", c=PASSES, u=2
            )
            for first, kind in ((0, ROPE), (2, CONTENT)):
                flipped = bank_tile(kind, b, [P, 2, 2, SEQ])
                for c in range(2):
                    for u in range(2):
                        nc.tensor.transpose(
                            flipped[:, c, u, :], x_words[:, first + c, u, :], identity[:]
                        )
                nc.scalar.copy(
                    out=grouped_words[:, first : first + 2],
                    in_=flipped[:].rearrange("p c u r -> p c r u"),
                )
            nc.vector.quantize_mx(
                out=x_codes[:, b].rearrange("p c r -> p (c r)").bitcast(FP8X4),
                scales=x_scales[:, b].rearrange("p c r -> p (c r)"),
                in_=x_grouped[:],
            )
        multiply_what_can_be(0)

        for unit in units[HEAD_UNITS : HEAD_UNITS + REGROUP_AHEAD]:
            regroup(unit, [])
        for step in range(HEAD_UNITS, len(units) + max(EMPTY_AFTER[ROPE], EMPTY_AFTER[CONTENT])):
            due = banks_due(step)
            if step + REGROUP_AHEAD < len(units):
                regroup(units[step + REGROUP_AHEAD], [tile[1] for tile, b in due])
            if step < len(units):
                quantise(units[step])
            content_banks = 0
            for tile, b in due:
                by_vector = step >= len(units) and content_banks % 2 == 1
                empty_bank(tile, b, nc.vector.tensor_copy if by_vector else nc.scalar.copy)
                emptied.add((tile, b))
                if tile[1] == CONTENT:
                    content_banks += 1
            multiply_what_can_be(step)
        assert not pending and len(emptied) == len(full)
